import numpy as np
import ml_dtypes

BF16 = ml_dtypes.bfloat16


def bf(x):
    return np.asarray(x, np.float32).astype(BF16)


def f32(x):
    return np.asarray(x, np.float32)


def f64(x):
    return np.asarray(x).astype(np.float64)


def striped(idx):
    return np.tile(idx.reshape(-1, 16).T, (8, 1))


C, S, K, N, H, R = 128, 1024, 4, 4096, 512, 8
SLOPE = 0.2


def lrelu(v):
    return np.maximum(v, 0.0) + SLOPE * np.minimum(v, 0.0)


def setup_inputs():
    x = f32(np.random.standard_normal((C, S)))
    a = f32(1.5 * np.random.standard_normal((C, K)) / np.sqrt(C))
    idx = np.concatenate([np.random.permutation(S)[:H] for _ in range(R)])
    return {"x": x, "a": a, "offs": striped(idx)}


def reference(x, a, offs):
    idx = offs[:16].T.reshape(-1)
    x = f64(x)
    a = f64(a)
    q = (x[:, :, None] * a[:, None, :]).reshape(C, N)
    p = x[:, idx] * q
    e = lrelu(p.sum(axis=0))
    w = np.exp(e).reshape(S, K)
    alpha = (w / w.sum(axis=1, keepdims=True)).reshape(1, N)
    return (x[:, idx] * alpha).reshape(C, S, K).sum(axis=2)

@@ -1,0 +1,107 @@
+import concourse.mybir as mybir
+from concourse.masks import make_identity
+
+F32 = mybir.dt.float32
+BF16 = mybir.dt.bfloat16
+U16 = mybir.dt.uint16
+ALU = mybir.AluOpType
+ACT = mybir.ActivationFunctionType
+X_AXIS = mybir.AxisListType.X
+
+C = 128
+S = 1024
+K = 4
+N = S * K
+SLOPE = 0.2
+
+NODES = 128
+PIECE = NODES * K
+PIECES = N // PIECE
+COLS = PIECE // 16
+GROUP = 2
+PARTS = 4
+
+FLOPS = 5 * C * N
+
+
+def tile_combinegraph_kernel(tc, x, a, offs, out):
+    nc = tc.nc
+    with (
+        tc.tile_pool(name="held", bufs=1) as held,
+        tc.tile_pool(name="pieces", bufs=PIECES) as pieces,
+        tc.tile_pool(name="small", bufs=2) as small,
+        tc.psum_pool(name="score_psum", bufs=2) as score_psum,
+        tc.psum_pool(name="spread_psum", bufs=2) as spread_psum,
+        tc.psum_pool(name="sum_psum", bufs=2) as sum_psum,
+    ):
+        offsets = held.tile([C, N // 16], U16, name="offsets")
+        nc.sync.dma_start(offsets[:], offs)
+        table = held.tile([C, S], F32, name="table")
+        for part in range(PARTS):
+            queue = nc.scalar if part % 2 == 0 else nc.sync
+            columns = slice(part * (S // PARTS), (part + 1) * (S // PARTS))
+            queue.dma_start(table[:, columns], x[:, columns])
+        a_sb = held.tile([C, K], F32, name="a_sb")
+        nc.gpsimd.dma_start(a_sb[:], a)
+        identity = held.tile([C, C], F32, name="identity")
+        make_identity(nc, identity[:])
+        ones = held.tile([C, 1], BF16, name="ones")
+        nc.vector.memset(ones[:], 1.0)
+
+        def looked_up(k):
+            return table[:].indirect(offsets[:, k * COLS : (k + 1) * COLS])
+
+        weights = []
+        for g in range(PIECES // GROUP):
+            scores = score_psum.tile([C, GROUP, K], F32, name="scores")
+            for h in range(GROUP):
+                k = g * GROUP + h
+                q = pieces.tile([C, NODES, K], F32, name="q")
+                nc.vector.tensor_tensor(
+                    q[:],
+                    table[:, k * NODES : (k + 1) * NODES].unsqueeze(2).to_broadcast([C, NODES, K]),
+                    a_sb[:].unsqueeze(1).to_broadcast([C, NODES, K]),
+                    ALU.mult,
+                )
+                p = pieces.tile([C, NODES, K], F32, name="p")
+                nc.vector.tensor_tensor(p[:], looked_up(k), q[:], ALU.mult)
+                p_bf = pieces.tile([C, NODES, K], BF16, name="p_bf")
+                nc.scalar.activation(p_bf[:], p[:], ACT.Copy)
+                for t in range(K):
+                    nc.tensor.matmul(scores[:, h, t : t + 1], lhsT=p_bf[:, :, t], rhs=ones[:], start=True, stop=True)
+
+            leak = small.tile([C, GROUP, K], F32, name="leak")
+            nc.scalar.mul(leak[:], scores[:], SLOPE)
+            e = small.tile([C, GROUP, K], F32, name="e")
+            nc.vector.tensor_tensor(e[:], scores[:], leak[:], ALU.max)
+            minus_top = small.tile([C, GROUP], F32, name="minus_top")
+            nc.vector.reduce_max(minus_top[:], e[:], axis=X_AXIS, negate=True)
+            w = small.tile([C, GROUP, K], F32, name="w")
+            total = small.tile([C, GROUP], F32, name="total")
+            for h in range(GROUP):
+                nc.scalar.activation(
+                    w[:, h, :], e[:, h, :], ACT.Exp, bias=minus_top[:, h : h + 1], accum_out=total[:, h : h + 1]
+                )
+            inverse = small.tile([C, GROUP], F32, name="inverse")
+            nc.vector.reciprocal(inverse[:], total[:])
+            alpha = small.tile([C, GROUP, K], F32, name="alpha")
+            for h in range(GROUP):
+                nc.scalar.mul(alpha[:, h, :], w[:, h, :], inverse[:, h : h + 1])
+
+            for h in range(GROUP):
+                spread = spread_psum.tile([C, K, NODES], F32, name="spread")
+                for t in range(K):
+                    nc.tensor.transpose(spread[:, t, :], alpha[:, h, t : t + 1].to_broadcast([C, C]), identity[:])
+                weight = pieces.tile([C, NODES, K], F32, name="weight")
+                nc.scalar.activation(weight[:], spread[:].rearrange("c t i -> c i t"), ACT.Copy)
+                weights.append(weight)
+
+        for k in range(PIECES):
+            r = pieces.tile([C, NODES, K], F32, name="r")
+            nc.vector.tensor_tensor(r[:], looked_up(k), weights[k][:], ALU.mult)
+            acc = sum_psum.tile([C, NODES], F32, name="acc")
+            for t in range(K):
+                nc.tensor.matmul(acc[:], lhsT=identity[:], rhs=r[:, :, t], start=(t == 0), stop=(t == K - 1))
+            result = pieces.tile([C, NODES], F32, name="result")
+            nc.scalar.activation(result[:], acc[:], ACT.Copy)
+            nc.sync.dma_start(out[:, k * NODES : (k + 1) * NODES], result[:])

@@ -33,6 +33,7 @@ def tile_combinegraph_kernel(tc, x, a, offs, out):
         tc.psum_pool(name="score_psum", bufs=2) as score_psum,
         tc.psum_pool(name="spread_psum", bufs=2) as spread_psum,
         tc.psum_pool(name="sum_psum", bufs=2) as sum_psum,
+        tc.psum_pool(name="back_psum", bufs=2) as back_psum,
     ):
         offsets = held.tile([C, N // 16], U16, name="offsets")
         nc.sync.dma_start(offsets[:], offs)
@@ -99,9 +100,15 @@ def tile_combinegraph_kernel(tc, x, a, offs, out):
         for k in range(PIECES):
             r = pieces.tile([C, NODES, K], F32, name="r")
             nc.vector.tensor_tensor(r[:], looked_up(k), weights[k][:], ALU.mult)
-            acc = sum_psum.tile([C, NODES], F32, name="acc")
+            flipped_sum = sum_psum.tile([NODES, C], F32, name="flipped_sum")
             for t in range(K):
-                nc.tensor.matmul(acc[:], lhsT=identity[:], rhs=r[:, :, t], start=(t == 0), stop=(t == K - 1))
+                nc.tensor.matmul(
+                    flipped_sum[:], lhsT=r[:, :, t], rhs=identity[:], is_transpose=True, start=(t == 0), stop=(t == K - 1)
+                )
+            flipped = pieces.tile([NODES, C], F32, name="flipped")
+            nc.scalar.activation(flipped[:], flipped_sum[:], ACT.Copy)
+            back = back_psum.tile([C, NODES], F32, name="back")
+            nc.tensor.transpose(back[:], flipped[:], identity[:])
             result = pieces.tile([C, NODES], F32, name="result")
-            nc.scalar.activation(result[:], acc[:], ACT.Copy)
+            nc.scalar.activation(result[:], back[:], ACT.Copy)
             nc.sync.dma_start(out[:, k * NODES : (k + 1) * NODES], result[:])

@@ -35,15 +35,15 @@ def tile_combinegraph_kernel(tc, x, a, offs, out):
         tc.psum_pool(name="sum_psum", bufs=2) as sum_psum,
         tc.psum_pool(name="back_psum", bufs=2) as back_psum,
     ):
-        offsets = held.tile([C, N // 16], U16, name="offsets")
-        nc.sync.dma_start(offsets[:], offs)
+        a_sb = held.tile([C, K], F32, name="a_sb")
+        nc.sync.dma_start(a_sb[:], a)
         table = held.tile([C, S], F32, name="table")
         for part in range(PARTS):
             queue = nc.scalar if part % 2 == 0 else nc.sync
             columns = slice(part * (S // PARTS), (part + 1) * (S // PARTS))
             queue.dma_start(table[:, columns], x[:, columns])
-        a_sb = held.tile([C, K], F32, name="a_sb")
-        nc.gpsimd.dma_start(a_sb[:], a)
+        offsets = held.tile([C, N // 16], U16, name="offsets")
+        nc.sync.dma_start(offsets[:], offs)
         identity = held.tile([C, C], F32, name="identity")
         make_identity(nc, identity[:])
         ones = held.tile([C, 1], BF16, name="ones")
@@ -100,15 +100,18 @@ def tile_combinegraph_kernel(tc, x, a, offs, out):
         for k in range(PIECES):
             r = pieces.tile([C, NODES, K], F32, name="r")
             nc.vector.tensor_tensor(r[:], looked_up(k), weights[k][:], ALU.mult)
-            flipped_sum = sum_psum.tile([NODES, C], F32, name="flipped_sum")
-            for t in range(K):
-                nc.tensor.matmul(
-                    flipped_sum[:], lhsT=r[:, :, t], rhs=identity[:], is_transpose=True, start=(t == 0), stop=(t == K - 1)
-                )
-            flipped = pieces.tile([NODES, C], F32, name="flipped")
-            nc.scalar.activation(flipped[:], flipped_sum[:], ACT.Copy)
-            back = back_psum.tile([C, NODES], F32, name="back")
-            nc.tensor.transpose(back[:], flipped[:], identity[:])
             result = pieces.tile([C, NODES], F32, name="result")
-            nc.scalar.activation(result[:], back[:], ACT.Copy)
+            if k < PIECES - GROUP:
+                flipped_sum = sum_psum.tile([NODES, C], F32, name="flipped_sum")
+                for t in range(K):
+                    nc.tensor.matmul(
+                        flipped_sum[:], lhsT=r[:, :, t], rhs=identity[:], is_transpose=True, start=(t == 0), stop=(t == K - 1)
+                    )
+                flipped = pieces.tile([NODES, C], F32, name="flipped")
+                nc.scalar.activation(flipped[:], flipped_sum[:], ACT.Copy)
+                back = back_psum.tile([C, NODES], F32, name="back")
+                nc.tensor.transpose(back[:], flipped[:], identity[:])
+                nc.scalar.activation(result[:], back[:], ACT.Copy)
+            else:
+                nc.vector.reduce_sum(result[:], r[:], axis=X_AXIS)
             nc.sync.dma_start(out[:, k * NODES : (k + 1) * NODES], result[:])

@@ -19,7 +19,7 @@ PIECE = NODES * K
 PIECES = N // PIECE
 COLS = PIECE // 16
 GROUP = 2
-PARTS = 4
+FIRST = GROUP * NODES
 
 FLOPS = 5 * C * N
 
@@ -37,13 +37,11 @@ def tile_combinegraph_kernel(tc, x, a, offs, out):
     ):
         a_sb = held.tile([C, K], F32, name="a_sb")
         nc.sync.dma_start(a_sb[:], a)
-        table = held.tile([C, S], F32, name="table")
-        for part in range(PARTS):
-            queue = nc.scalar if part % 2 == 0 else nc.sync
-            columns = slice(part * (S // PARTS), (part + 1) * (S // PARTS))
-            queue.dma_start(table[:, columns], x[:, columns])
         offsets = held.tile([C, N // 16], U16, name="offsets")
         nc.sync.dma_start(offsets[:], offs)
+        table = held.tile([C, S], F32, name="table")
+        nc.scalar.dma_start(table[:, :FIRST], x[:, :FIRST])
+        nc.scalar.dma_start(table[:, FIRST:], x[:, FIRST:])
         identity = held.tile([C, C], F32, name="identity")
         make_identity(nc, identity[:])
         ones = held.tile([C, 1], BF16, name="ones")
@@ -71,12 +69,13 @@ def tile_combinegraph_kernel(tc, x, a, offs, out):
                 for t in range(K):
                     nc.tensor.matmul(scores[:, h, t : t + 1], lhsT=p_bf[:, :, t], rhs=ones[:], start=True, stop=True)
 
-            leak = small.tile([C, GROUP, K], F32, name="leak")
-            nc.scalar.mul(leak[:], scores[:], SLOPE)
+            both = small.tile([C, GROUP, 2, K], F32, name="both")
+            nc.scalar.activation(both[:, :, 0, :], scores[:], ACT.Copy)
+            nc.scalar.mul(both[:, :, 1, :], scores[:], SLOPE)
             e = small.tile([C, GROUP, K], F32, name="e")
-            nc.vector.tensor_tensor(e[:], scores[:], leak[:], ALU.max)
+            nc.vector.reduce_max(e[:], both[:].rearrange("i h s t -> i h t s"), axis=X_AXIS)
             minus_top = small.tile([C, GROUP], F32, name="minus_top")
-            nc.vector.reduce_max(minus_top[:], e[:], axis=X_AXIS, negate=True)
+            nc.vector.reduce_max(minus_top[:], both[:].rearrange("i h s t -> i h (s t)"), axis=X_AXIS, negate=True)
             w = small.tile([C, GROUP, K], F32, name="w")
             total = small.tile([C, GROUP], F32, name="total")
             for h in range(GROUP):

@@ -19,6 +19,8 @@ PIECE = NODES * K
 PIECES = N // PIECE
 COLS = PIECE // 16
 GROUP = 2
+SCALAR_Q = 2
+AHEAD = 4
 FIRST = GROUP * NODES
 
 FLOPS = 5 * C * N
@@ -29,6 +31,7 @@ def tile_combinegraph_kernel(tc, x, a, offs, out):
     with (
         tc.tile_pool(name="held", bufs=1) as held,
         tc.tile_pool(name="pieces", bufs=PIECES) as pieces,
+        tc.tile_pool(name="ahead", bufs=AHEAD) as ahead,
         tc.tile_pool(name="small", bufs=2) as small,
         tc.psum_pool(name="score_psum", bufs=2) as score_psum,
         tc.psum_pool(name="spread_psum", bufs=2) as spread_psum,
@@ -44,43 +47,60 @@ def tile_combinegraph_kernel(tc, x, a, offs, out):
         nc.scalar.dma_start(table[:, FIRST:], x[:, FIRST:])
         identity = held.tile([C, C], F32, name="identity")
         make_identity(nc, identity[:])
-        ones = held.tile([C, 1], BF16, name="ones")
-        nc.vector.memset(ones[:], 1.0)
+        one_and_five = held.tile([C, 2], BF16, name="one_and_five")
+        nc.vector.memset(one_and_five[:, 0:1], 1.0)
+        nc.vector.memset(one_and_five[:, 1:2], 1.0 / SLOPE)
+
+        warm = held.tile([C, 2], F32, name="warm")
+        nc.scalar.activation(warm[:], one_and_five[:], ACT.Exp)
+
+        late = (PIECES - SCALAR_Q) * NODES
+        by_type = held.tile([C, K, S - late], F32, name="by_type")
+        for t in range(K):
+            nc.scalar.mul(by_type[:, t, :], table[:, late:], a_sb[:, t : t + 1])
 
         def looked_up(k):
             return table[:].indirect(offsets[:, k * COLS : (k + 1) * COLS])
 
         weights = []
         for g in range(PIECES // GROUP):
-            scores = score_psum.tile([C, GROUP, K], F32, name="scores")
+            scores = score_psum.tile([C, GROUP, K, 2], F32, name="scores")
             for h in range(GROUP):
                 k = g * GROUP + h
-                q = pieces.tile([C, NODES, K], F32, name="q")
-                nc.vector.tensor_tensor(
-                    q[:],
-                    table[:, k * NODES : (k + 1) * NODES].unsqueeze(2).to_broadcast([C, NODES, K]),
-                    a_sb[:].unsqueeze(1).to_broadcast([C, NODES, K]),
-                    ALU.mult,
-                )
+                q = ahead.tile([C, NODES, K], F32, name="q")
+                if k * NODES < late:
+                    nc.vector.tensor_tensor(
+                        q[:],
+                        table[:, k * NODES : (k + 1) * NODES].unsqueeze(2).to_broadcast([C, NODES, K]),
+                        a_sb[:].unsqueeze(1).to_broadcast([C, NODES, K]),
+                        ALU.mult,
+                    )
+                else:
+                    rows = by_type[:, :, k * NODES - late : (k + 1) * NODES - late]
+                    nc.scalar.activation(q[:], rows.rearrange("c t i -> c i t"), ACT.Copy)
                 p = pieces.tile([C, NODES, K], F32, name="p")
                 nc.vector.tensor_tensor(p[:], looked_up(k), q[:], ALU.mult)
                 p_bf = pieces.tile([C, NODES, K], BF16, name="p_bf")
                 nc.scalar.activation(p_bf[:], p[:], ACT.Copy)
                 for t in range(K):
-                    nc.tensor.matmul(scores[:, h, t : t + 1], lhsT=p_bf[:, :, t], rhs=ones[:], start=True, stop=True)
+                    nc.tensor.matmul(scores[:, h, t, :], lhsT=p_bf[:, :, t], rhs=one_and_five[:], start=True, stop=True)
 
-            both = small.tile([C, GROUP, 2, K], F32, name="both")
-            nc.scalar.activation(both[:, :, 0, :], scores[:], ACT.Copy)
-            nc.scalar.mul(both[:, :, 1, :], scores[:], SLOPE)
-            e = small.tile([C, GROUP, K], F32, name="e")
-            nc.vector.reduce_max(e[:], both[:].rearrange("i h s t -> i h t s"), axis=X_AXIS)
+            five_e = small.tile([C, GROUP, K], F32, name="five_e")
+            nc.vector.reduce_max(five_e[:], scores[:], axis=X_AXIS)
+            minus_five_top = small.tile([C, GROUP], F32, name="minus_five_top")
+            nc.vector.reduce_max(minus_five_top[:], scores[:].rearrange("i h t s -> i h (t s)"), axis=X_AXIS, negate=True)
             minus_top = small.tile([C, GROUP], F32, name="minus_top")
-            nc.vector.reduce_max(minus_top[:], both[:].rearrange("i h s t -> i h (s t)"), axis=X_AXIS, negate=True)
+            nc.scalar.mul(minus_top[:], minus_five_top[:], SLOPE)
             w = small.tile([C, GROUP, K], F32, name="w")
             total = small.tile([C, GROUP], F32, name="total")
             for h in range(GROUP):
                 nc.scalar.activation(
-                    w[:, h, :], e[:, h, :], ACT.Exp, bias=minus_top[:, h : h + 1], accum_out=total[:, h : h + 1]
+                    w[:, h, :],
+                    five_e[:, h, :],
+                    ACT.Exp,
+                    scale=SLOPE,
+                    bias=minus_top[:, h : h + 1],
+                    accum_out=total[:, h : h + 1],
                 )
             inverse = small.tile([C, GROUP], F32, name="inverse")
             nc.vector.reciprocal(inverse[:], total[:])

@@ -19,8 +19,8 @@ PIECE = NODES * K
 PIECES = N // PIECE
 COLS = PIECE // 16
 GROUP = 2
-SCALAR_Q = 2
-AHEAD = 4
+SCALAR_Q = 3
+AHEAD = 2
 FIRST = GROUP * NODES
 
 FLOPS = 5 * C * N
@@ -31,7 +31,7 @@ def tile_combinegraph_kernel(tc, x, a, offs, out):
     with (
         tc.tile_pool(name="held", bufs=1) as held,
         tc.tile_pool(name="pieces", bufs=PIECES) as pieces,
-        tc.tile_pool(name="ahead", bufs=AHEAD) as ahead,
+        tc.tile_pool(name="ahead", bufs=AHEAD + 1) as ahead,
         tc.tile_pool(name="small", bufs=2) as small,
         tc.psum_pool(name="score_psum", bufs=2) as score_psum,
         tc.psum_pool(name="spread_psum", bufs=2) as spread_psum,
@@ -59,27 +59,33 @@ def tile_combinegraph_kernel(tc, x, a, offs, out):
         for t in range(K):
             nc.scalar.mul(by_type[:, t, :], table[:, late:], a_sb[:, t : t + 1])
 
+        def make_q(k):
+            q = ahead.tile([C, NODES, K], F32, name="q")
+            if k * NODES < late:
+                nc.vector.tensor_tensor(
+                    q[:],
+                    table[:, k * NODES : (k + 1) * NODES].unsqueeze(2).to_broadcast([C, NODES, K]),
+                    a_sb[:].unsqueeze(1).to_broadcast([C, NODES, K]),
+                    ALU.mult,
+                )
+            else:
+                rows = by_type[:, :, k * NODES - late : (k + 1) * NODES - late]
+                nc.scalar.activation(q[:], rows.rearrange("c t i -> c i t"), ACT.Copy)
+            return q
+
         def looked_up(k):
             return table[:].indirect(offsets[:, k * COLS : (k + 1) * COLS])
 
+        qs = [make_q(k) for k in range(AHEAD)]
         weights = []
         for g in range(PIECES // GROUP):
             scores = score_psum.tile([C, GROUP, K, 2], F32, name="scores")
             for h in range(GROUP):
                 k = g * GROUP + h
-                q = ahead.tile([C, NODES, K], F32, name="q")
-                if k * NODES < late:
-                    nc.vector.tensor_tensor(
-                        q[:],
-                        table[:, k * NODES : (k + 1) * NODES].unsqueeze(2).to_broadcast([C, NODES, K]),
-                        a_sb[:].unsqueeze(1).to_broadcast([C, NODES, K]),
-                        ALU.mult,
-                    )
-                else:
-                    rows = by_type[:, :, k * NODES - late : (k + 1) * NODES - late]
-                    nc.scalar.activation(q[:], rows.rearrange("c t i -> c i t"), ACT.Copy)
                 p = pieces.tile([C, NODES, K], F32, name="p")
-                nc.vector.tensor_tensor(p[:], looked_up(k), q[:], ALU.mult)
+                nc.vector.tensor_tensor(p[:], looked_up(k), qs[k][:], ALU.mult)
+                if k + AHEAD < PIECES:
+                    qs.append(make_q(k + AHEAD))
                 p_bf = pieces.tile([C, NODES, K], BF16, name="p_bf")
                 nc.scalar.activation(p_bf[:], p[:], ACT.Copy)
                 for t in range(K):

@@ -18,10 +18,11 @@ NODES = 128
 PIECE = NODES * K
 PIECES = N // PIECE
 COLS = PIECE // 16
-GROUP = 2
+GROUPS = (2, 2, 1, 1, 1, 1)
+VECTOR_SUMS = 2
 SCALAR_Q = 3
 AHEAD = 2
-FIRST = GROUP * NODES
+FIRST = GROUPS[0] * NODES
 
 FLOPS = 5 * C * N
 
@@ -78,10 +79,10 @@ def tile_combinegraph_kernel(tc, x, a, offs, out):
 
         qs = [make_q(k) for k in range(AHEAD)]
         weights = []
-        for g in range(PIECES // GROUP):
-            scores = score_psum.tile([C, GROUP, K, 2], F32, name="scores")
-            for h in range(GROUP):
-                k = g * GROUP + h
+        for size in GROUPS:
+            scores = score_psum.tile([C, size, K, 2], F32, name="scores")
+            for h in range(size):
+                k = len(weights) + h
                 p = pieces.tile([C, NODES, K], F32, name="p")
                 nc.vector.tensor_tensor(p[:], looked_up(k), qs[k][:], ALU.mult)
                 if k + AHEAD < PIECES:
@@ -91,15 +92,15 @@ def tile_combinegraph_kernel(tc, x, a, offs, out):
                 for t in range(K):
                     nc.tensor.matmul(scores[:, h, t, :], lhsT=p_bf[:, :, t], rhs=one_and_five[:], start=True, stop=True)
 
-            five_e = small.tile([C, GROUP, K], F32, name="five_e")
+            five_e = small.tile([C, size, K], F32, name="five_e")
             nc.vector.reduce_max(five_e[:], scores[:], axis=X_AXIS)
-            minus_five_top = small.tile([C, GROUP], F32, name="minus_five_top")
+            minus_five_top = small.tile([C, size], F32, name="minus_five_top")
             nc.vector.reduce_max(minus_five_top[:], scores[:].rearrange("i h t s -> i h (t s)"), axis=X_AXIS, negate=True)
-            minus_top = small.tile([C, GROUP], F32, name="minus_top")
+            minus_top = small.tile([C, size], F32, name="minus_top")
             nc.scalar.mul(minus_top[:], minus_five_top[:], SLOPE)
-            w = small.tile([C, GROUP, K], F32, name="w")
-            total = small.tile([C, GROUP], F32, name="total")
-            for h in range(GROUP):
+            w = small.tile([C, size, K], F32, name="w")
+            total = small.tile([C, size], F32, name="total")
+            for h in range(size):
                 nc.scalar.activation(
                     w[:, h, :],
                     five_e[:, h, :],
@@ -108,13 +109,13 @@ def tile_combinegraph_kernel(tc, x, a, offs, out):
                     bias=minus_top[:, h : h + 1],
                     accum_out=total[:, h : h + 1],
                 )
-            inverse = small.tile([C, GROUP], F32, name="inverse")
+            inverse = small.tile([C, size], F32, name="inverse")
             nc.vector.reciprocal(inverse[:], total[:])
-            alpha = small.tile([C, GROUP, K], F32, name="alpha")
-            for h in range(GROUP):
+            alpha = small.tile([C, size, K], F32, name="alpha")
+            for h in range(size):
                 nc.scalar.mul(alpha[:, h, :], w[:, h, :], inverse[:, h : h + 1])
 
-            for h in range(GROUP):
+            for h in range(size):
                 spread = spread_psum.tile([C, K, NODES], F32, name="spread")
                 for t in range(K):
                     nc.tensor.transpose(spread[:, t, :], alpha[:, h, t : t + 1].to_broadcast([C, C]), identity[:])
@@ -126,7 +127,7 @@ def tile_combinegraph_kernel(tc, x, a, offs, out):
             r = pieces.tile([C, NODES, K], F32, name="r")
             nc.vector.tensor_tensor(r[:], looked_up(k), weights[k][:], ALU.mult)
             result = pieces.tile([C, NODES], F32, name="result")
-            if k < PIECES - GROUP:
+            if k < PIECES - VECTOR_SUMS:
                 flipped_sum = sum_psum.tile([NODES, C], F32, name="flipped_sum")
                 for t in range(K):
                     nc.tensor.matmul(

import concourse.mybir as mybir
from concourse.masks import make_identity

F32 = mybir.dt.float32
BF16 = mybir.dt.bfloat16
U16 = mybir.dt.uint16
ALU = mybir.AluOpType
ACT = mybir.ActivationFunctionType
X_AXIS = mybir.AxisListType.X

C = 128
S = 1024
K = 4
N = S * K
SLOPE = 0.2

NODES = 128
PIECE = NODES * K
PIECES = N // PIECE
COLS = PIECE // 16
GROUPS = (2, 2, 1, 1, 1, 1)
VECTOR_SUMS = 2
SCALAR_Q = 3
AHEAD = 2
FIRST = GROUPS[0] * NODES

FLOPS = 5 * C * N


def tile_combinegraph_kernel(tc, x, a, offs, out):
    nc = tc.nc
    with (
        tc.tile_pool(name="held", bufs=1) as held,
        tc.tile_pool(name="pieces", bufs=PIECES) as pieces,
        tc.tile_pool(name="ahead", bufs=AHEAD + 1) as ahead,
        tc.tile_pool(name="small", bufs=2) as small,
        tc.psum_pool(name="score_psum", bufs=2) as score_psum,
        tc.psum_pool(name="spread_psum", bufs=2) as spread_psum,
        tc.psum_pool(name="sum_psum", bufs=2) as sum_psum,
        tc.psum_pool(name="back_psum", bufs=2) as back_psum,
    ):
        a_sb = held.tile([C, K], F32, name="a_sb")
        nc.sync.dma_start(a_sb[:], a)
        offsets = held.tile([C, N // 16], U16, name="offsets")
        nc.sync.dma_start(offsets[:], offs)
        table = held.tile([C, S], F32, name="table")
        nc.scalar.dma_start(table[:, :FIRST], x[:, :FIRST])
        nc.scalar.dma_start(table[:, FIRST:], x[:, FIRST:])
        identity = held.tile([C, C], F32, name="identity")
        make_identity(nc, identity[:])
        one_and_five = held.tile([C, 2], BF16, name="one_and_five")
        nc.vector.memset(one_and_five[:, 0:1], 1.0)
        nc.vector.memset(one_and_five[:, 1:2], 1.0 / SLOPE)

        warm = held.tile([C, 2], F32, name="warm")
        nc.scalar.activation(warm[:], one_and_five[:], ACT.Exp)

        late = (PIECES - SCALAR_Q) * NODES
        by_type = held.tile([C, K, S - late], F32, name="by_type")
        for t in range(K):
            nc.scalar.mul(by_type[:, t, :], table[:, late:], a_sb[:, t : t + 1])

        def make_q(k):
            q = ahead.tile([C, NODES, K], F32, name="q")
            if k * NODES < late:
                nc.vector.tensor_tensor(
                    q[:],
                    table[:, k * NODES : (k + 1) * NODES].unsqueeze(2).to_broadcast([C, NODES, K]),
                    a_sb[:].unsqueeze(1).to_broadcast([C, NODES, K]),
                    ALU.mult,
                )
            else:
                rows = by_type[:, :, k * NODES - late : (k + 1) * NODES - late]
                nc.scalar.activation(q[:], rows.rearrange("c t i -> c i t"), ACT.Copy)
            return q

        def looked_up(k):
            return table[:].indirect(offsets[:, k * COLS : (k + 1) * COLS])

        qs = [make_q(k) for k in range(AHEAD)]
        weights = []
        for size in GROUPS:
            scores = score_psum.tile([C, size, K, 2], F32, name="scores")
            for h in range(size):
                k = len(weights) + h
                p = pieces.tile([C, NODES, K], F32, name="p")
                nc.vector.tensor_tensor(p[:], looked_up(k), qs[k][:], ALU.mult)
                if k + AHEAD < PIECES:
                    qs.append(make_q(k + AHEAD))
                p_bf = pieces.tile([C, NODES, K], BF16, name="p_bf")
                nc.scalar.activation(p_bf[:], p[:], ACT.Copy)
                for t in range(K):
                    nc.tensor.matmul(scores[:, h, t, :], lhsT=p_bf[:, :, t], rhs=one_and_five[:], start=True, stop=True)

            five_e = small.tile([C, size, K], F32, name="five_e")
            nc.vector.reduce_max(five_e[:], scores[:], axis=X_AXIS)
            minus_five_top = small.tile([C, size], F32, name="minus_five_top")
            nc.vector.reduce_max(minus_five_top[:], scores[:].rearrange("i h t s -> i h (t s)"), axis=X_AXIS, negate=True)
            minus_top = small.tile([C, size], F32, name="minus_top")
            nc.scalar.mul(minus_top[:], minus_five_top[:], SLOPE)
            w = small.tile([C, size, K], F32, name="w")
            total = small.tile([C, size], F32, name="total")
            for h in range(size):
                nc.scalar.activation(
                    w[:, h, :],
                    five_e[:, h, :],
                    ACT.Exp,
                    scale=SLOPE,
                    bias=minus_top[:, h : h + 1],
                    accum_out=total[:, h : h + 1],
                )
            inverse = small.tile([C, size], F32, name="inverse")
            nc.vector.reciprocal(inverse[:], total[:])
            alpha = small.tile([C, size, K], F32, name="alpha")
            for h in range(size):
                nc.scalar.mul(alpha[:, h, :], w[:, h, :], inverse[:, h : h + 1])

            for h in range(size):
                spread = spread_psum.tile([C, K, NODES], F32, name="spread")
                for t in range(K):
                    nc.tensor.transpose(spread[:, t, :], alpha[:, h, t : t + 1].to_broadcast([C, C]), identity[:])
                weight = pieces.tile([C, NODES, K], F32, name="weight")
                nc.scalar.activation(weight[:], spread[:].rearrange("c t i -> c i t"), ACT.Copy)
                weights.append(weight)

        for k in range(PIECES):
            r = pieces.tile([C, NODES, K], F32, name="r")
            nc.vector.tensor_tensor(r[:], looked_up(k), weights[k][:], ALU.mult)
            result = pieces.tile([C, NODES], F32, name="result")
            if k < PIECES - VECTOR_SUMS:
                flipped_sum = sum_psum.tile([NODES, C], F32, name="flipped_sum")
                for t in range(K):
                    nc.tensor.matmul(
                        flipped_sum[:], lhsT=r[:, :, t], rhs=identity[:], is_transpose=True, start=(t == 0), stop=(t == K - 1)
                    )
                flipped = pieces.tile([NODES, C], F32, name="flipped")
                nc.scalar.activation(flipped[:], flipped_sum[:], ACT.Copy)
                back = back_psum.tile([C, NODES], F32, name="back")
                nc.tensor.transpose(back[:], flipped[:], identity[:])
                nc.scalar.activation(result[:], back[:], ACT.Copy)
            else:
                nc.vector.reduce_sum(result[:], r[:], axis=X_AXIS)
            nc.sync.dma_start(out[:, k * NODES : (k + 1) * NODES], result[:])
